import numpy as np
import ml_dtypes


def mxq(x, axis, fmt="e4m3"):
    dtype, down = {"e4m3": (ml_dtypes.float8_e4m3fn, 7), "e5m2": (ml_dtypes.float8_e5m2, 14)}[fmt]
    v = np.moveaxis(np.asarray(x, np.float32).astype(ml_dtypes.bfloat16).astype(np.float64), axis, -1)
    blocks = v.reshape(v.shape[:-1] + (-1, 32))
    amax = np.abs(blocks).max(-1, keepdims=True)
    byte = np.maximum(np.where(amax > 0, np.frexp(amax)[1] - 1 + 127, 0) - down, 1)
    scale = np.exp2(byte - 127.0)
    codes = (blocks / scale).astype(np.float32).astype(dtype).astype(np.float64)
    return np.moveaxis((codes * scale).reshape(v.shape), -1, axis)


WIDE = False


def mx_kscale(k):
    if not WIDE:
        return np.ones(k)
    levels = np.array([10, -10, 5, -5, 0])
    a = np.random.permutation(np.resize(levels, k // 512 * 4)).reshape(k // 512, 4)
    idx = np.arange(k)
    return np.exp2(a[idx // 512, idx % 128 // 32])


BF16 = ml_dtypes.bfloat16


def bf(x):
    return np.asarray(x, np.float32).astype(BF16)


def f64(x):
    return np.asarray(x).astype(np.float64)


E2M1 = np.array([0.0, 0.5, 1.0, 1.5, 2.0, 3.0, 4.0, 6.0, -0.0, -0.5, -1.0, -1.5, -2.0, -3.0, -4.0, -6.0])


def pack_weight(w, fmt):
    k, n = w.shape
    w = f64(bf(w)).reshape(k // 32, 32, n)
    amax = np.abs(w).max(1)
    if fmt == "e4m3":
        byte = np.frexp(amax)[1] - 1 + 127 - 7
    else:
        mant, ex = np.frexp(amax / 6.0)
        byte = np.where(mant > 0.5, ex, ex - 1) + 127
    byte = np.clip(np.where(amax > 0, byte, 1), 1, 254)
    scaled = (w * np.exp2(127.0 - byte)[:, None, :]).reshape(k, n).astype(np.float32)
    by_word = np.ascontiguousarray(scaled.reshape(k // 512, 128, 4, n).transpose(0, 1, 3, 2))
    if fmt == "e4m3":
        words = by_word.astype(ml_dtypes.float8_e4m3fn).view(np.uint8)
    else:
        c = by_word.astype(ml_dtypes.float4_e2m1fn).view(np.uint8) & 0xF
        words = c[..., 0::2] | (c[..., 1::2] << 4)
    return np.ascontiguousarray(words), np.ascontiguousarray(byte.astype(np.uint8).reshape(k // 512, 16, n))


def unpack_weight(words, scales, fmt):
    g, p, n, _ = words.shape
    if fmt == "e4m3":
        vals = np.ascontiguousarray(words).view(ml_dtypes.float8_e4m3fn).astype(np.float64)
    else:
        nib = np.empty((g, p, n, 4), np.uint8)
        nib[..., 0::2] = words & 0xF
        nib[..., 1::2] = words >> 4
        vals = E2M1[nib]
    vals = vals * np.repeat(np.exp2(scales.astype(np.float64) - 127.0), 8, axis=1)[..., None]
    return vals.transpose(0, 1, 3, 2).reshape(g * 512, n)


E, LMAX, MMAX, CIN, COUT = 128, 3, 2, 1024, 512
NS = [LMAX + 1 - m for m in range(MMAX + 1)]
NC = NS[0] + sum(2 * n for n in NS[1:])
FMT = "e4m3"


def setup_inputs():
    ss = [mx_kscale(n * CIN) for n in NS]
    sx = np.concatenate([ss[0].reshape(NS[0], CIN)] + [np.tile(ss[m].reshape(NS[m], CIN), (2, 1)) for m in range(1, MMAX + 1)], axis=0)
    x = np.random.standard_normal((E, NC, CIN)) * sx
    W0 = np.random.standard_normal((NS[0] * COUT, NS[0] * CIN)) / np.sqrt(NS[0] * CIN) / ss[0][None, :]
    b0 = np.random.standard_normal(NS[0] * COUT) * 0.3
    W1 = np.random.standard_normal((2 * NS[1] * COUT, NS[1] * CIN)) / (np.sqrt(2.0) * np.sqrt(NS[1] * CIN)) / ss[1][None, :]
    W2 = np.random.standard_normal((2 * NS[2] * COUT, NS[2] * CIN)) / (np.sqrt(2.0) * np.sqrt(NS[2] * CIN)) / ss[2][None, :]
    W0_words, W0_scales = pack_weight(np.ascontiguousarray(W0.T), FMT)
    W1_words, W1_scales = pack_weight(np.ascontiguousarray(W1.T), FMT)
    W2_words, W2_scales = pack_weight(np.ascontiguousarray(W2.T), FMT)
    return {"x": bf(x), "W0_words": W0_words, "W0_scales": W0_scales, "b0": bf(b0), "W1_words": W1_words, "W1_scales": W1_scales, "W2_words": W2_words, "W2_scales": W2_scales}


def reference(x, W0_words, W0_scales, b0, W1_words, W1_scales, W2_words, W2_scales):
    x = f64(x)
    WmT = [unpack_weight(W1_words, W1_scales, FMT), unpack_weight(W2_words, W2_scales, FMT)]
    outs = []
    x0 = x[:, :LMAX + 1].reshape(E, (LMAX + 1) * CIN)
    y0 = (mxq(x0, 1, "e4m3") @ unpack_weight(W0_words, W0_scales, FMT)) + f64(b0)
    outs.append(y0.reshape(E, LMAX + 1, COUT))
    offset = LMAX + 1
    for m in range(1, MMAX + 1):
        n = LMAX + 1 - m
        xm = x[:, offset:offset + 2 * n].reshape(E, 2, n * CIN)
        offset += 2 * n
        ym = mxq(xm, 2, "e4m3") @ WmT[m - 1]
        of = n * COUT
        x_r, x_i = ym[..., :of], ym[..., of:]
        pos = x_r[:, 0] - x_i[:, 1]
        neg = x_r[:, 1] + x_i[:, 0]
        outs.append(pos.reshape(E, n, COUT))
        outs.append(neg.reshape(E, n, COUT))
    return np.concatenate(outs, axis=1)

@@ -1,0 +1,186 @@
+from contextlib import ExitStack
+
+import concourse.mybir as mybir
+from concourse.masks import make_identity
+
+F32 = mybir.dt.float32
+BF16 = mybir.dt.bfloat16
+I32 = mybir.dt.int32
+U32 = mybir.dt.uint32
+U8 = mybir.dt.uint8
+FP8X4 = mybir.dt.float8_e4m3fn_x4
+
+P = 128
+NT = 512
+FLOPS = 2 * 128 * (4096 * 2048 + 2 * 3072 * 3072 + 2 * 2048 * 2048)
+
+
+def tile_so2linear_w_kernel(tc, x, W0_words, W0_scales, b0, W1_words, W1_scales, W2_words, W2_scales, out):
+    nc = tc.nc
+    with ExitStack() as ctx:
+        ctx.enter_context(tc.manual_schedule())
+        keep = ctx.enter_context(tc.tile_pool(name="keep", bufs=1))
+        stage = ctx.enter_context(tc.tile_pool(name="stage", bufs=4))
+        wpool = ctx.enter_context(tc.tile_pool(name="wpool", bufs=8))
+        psum = ctx.enter_context(tc.psum_pool(name="psum", bufs=1))
+
+        def bank(b, label):
+            return psum.tile([P, NT], F32, tag="bank%d" % b, name="bk_%s" % label)
+
+        ident = keep.tile([P, P], F32, name="ident")
+        make_identity(nc, ident[:])
+        brow = keep.tile([P, 2048], BF16, name="brow")
+        nc.vector.memset(brow[:].bitcast(I32), 0)
+        ones = keep.tile([P, P], BF16, name="ones")
+        nc.vector.memset(ones[:], 1.0)
+        nc.scalar.dma_start(out=brow[0:1, :], in_=b0.rearrange("(o n) -> o n", o=1))
+
+        plane_specs = [
+            ("w1a", W1_scales, 0, 4, 3072),
+            ("w1b", W1_scales, 4, 2, 3072),
+            ("w2a", W2_scales, 0, 4, 2048),
+            ("w0a", W0_scales, 0, 4, 2048),
+            ("w0b", W0_scales, 4, 4, 2048),
+        ]
+        planes = {}
+        for label, src, g0, ng, n in plane_specs:
+            pl = keep.tile([P, n], U8, name="pl_%s" % label, align_bytes=64)
+            nc.vector.memset(pl[:].bitcast(I32), 0)
+            planes[label] = pl
+
+        pieces = [(4, 7), (7, 10), (10, 14), (0, 4)]
+        xp = []
+        for i, (c0, c1) in enumerate(pieces):
+            t = keep.tile([P, (c1 - c0) * 1024], BF16, name="xp%d" % i)
+            nc.sync.dma_start(out=t[:], in_=x[:, c0:c1, :].rearrange("e c k -> e (c k)"))
+            xp.append(t)
+
+        for label, src, g0, ng, n in plane_specs:
+            pl = planes[label]
+            for q in range(4):
+                nc.sync.dma_start(
+                    out=pl[32 * q : 32 * q + 4 * ng, :].bitcast(I32),
+                    in_=src[g0 : g0 + ng, 4 * q : 4 * q + 4, :].bitcast(I32),
+                )
+
+        def load_w(words, g, n, label):
+            t = wpool.tile([P, 3072], U32, tag="w", name="w_%s" % label, align_bytes=64)
+            nc.sync.dma_start(
+                out=t[:, 0:n].bitcast(I32),
+                in_=words[g].rearrange("p n t -> p (n t)").bitcast(I32),
+            )
+            return t
+
+        w1 = [load_w(W1_words, g, 3072, "1_%d" % g) for g in range(6)]
+        w2 = [load_w(W2_words, g, 2048, "2_%d" % g) for g in range(4)]
+        w0 = [load_w(W0_words, g, 2048, "0_%d" % g) for g in range(7)]
+        w0_last = []
+        for j in range(4):
+            t = wpool.tile([P, NT], U32, tag="wl", bufs=4, name="wl_%d" % j, align_bytes=64)
+            nc.sync.dma_start(
+                out=t[:].bitcast(I32),
+                in_=W0_words[7].rearrange("p n t -> p (n t)")[:, 4 * NT * j : 4 * NT * (j + 1)].bitcast(I32),
+            )
+            w0_last.append(t)
+
+        bias = keep.tile([P, 2048], F32, name="bias")
+        for j in range(4):
+            bk = bank(4 + j, "bias%d" % j)
+            nc.tensor.matmul(out=bk[:], lhsT=ones[:], rhs=brow[:, NT * j : NT * (j + 1)], start=True, stop=True)
+            nc.scalar.copy(out=bias[:, NT * j : NT * (j + 1)], in_=bk[:])
+
+        n_slots = {1: 18, 2: 12, 0: 8}
+        xq = {}
+        xs = {}
+        for m in (1, 2, 0):
+            xq[m] = keep.tile([P, n_slots[m] * P], U32, name="xq%d" % m, align_bytes=64)
+            xs[m] = keep.tile([P, n_slots[m] * P], U8, name="xs%d" % m, align_bytes=64)
+
+        units = []
+        for l in range(0, 6, 2):
+            units.append((0, l, 1, l, None))
+        for l in range(0, 6, 2):
+            units.append((1, l, 1, 6 + l, 12 + l))
+        for l in range(0, 4, 2):
+            units.append((2, l, 2, l, None))
+        for l in range(4, 8, 2):
+            units.append((2, l, 2, l, 4 + l))
+        for l in range(0, 8, 2):
+            units.append((3, l, 0, l, None))
+
+        def quantise(m, slot, src):
+            nc.vector.quantize_mx(
+                out=xq[m][:, slot * P : (slot + 2) * P].bitcast(FP8X4),
+                scales=xs[m][:, slot * P : (slot + 2) * P],
+                in_=src[:],
+            )
+
+        for i, (pc, l, m, slot, nslot) in enumerate(units):
+            xw = xp[pc][:].bitcast(F32)
+            bk = bank(i % 8, "t%d" % i)
+            bk4 = bk[:].rearrange("p (j u e) -> p j u e", j=2, u=2)
+            for j in range(2):
+                for u in range(2):
+                    nc.tensor.transpose(bk4[:, j, u, :], xw[:, 256 * (l + j) + u : 256 * (l + j + 1) : 2], ident[:])
+            grp = stage.tile([P, 1024], BF16, tag="grp", name="grp%d" % i, align_bytes=64)
+            nc.scalar.copy(
+                out=grp[:].bitcast(F32).rearrange("p (j e u) -> p j e u", j=2, u=2),
+                in_=bk4.rearrange("p j u e -> p j e u"),
+            )
+            if nslot is not None:
+                neg = stage.tile([P, 1024], BF16, tag="neg", name="neg%d" % i, align_bytes=64)
+                nc.vector.tensor_scalar(out=neg[:], in0=grp[:], scalar1=-1.0, scalar2=None, op0=mybir.AluOpType.mult)
+            quantise(m, slot, grp)
+            if nslot is not None:
+                quantise(m, nslot, neg)
+
+        def mx(acc, m, slot, wt, wcol, pl, k, pcol, start, stop):
+            nc.tensor.matmul_mx(
+                out=acc[:],
+                lhsT=xq[m][:, slot * P : (slot + 1) * P].bitcast(FP8X4),
+                lhsT_scale=xs[m][:, slot * P : (slot + 1) * P],
+                rhs=wt[:, wcol : wcol + NT].bitcast(FP8X4),
+                rhs_scale=pl[k:P, pcol : pcol + NT],
+                start=start,
+                stop=stop,
+            )
+
+        def complex_phase(m, groups, nh, wts, plane_of, banks, comp0):
+            pos = [bank(banks[2 * j], "m%dpos%d" % (m, j)) for j in range(nh)]
+            neg = [bank(banks[2 * j + 1], "m%dneg%d" % (m, j)) for j in range(nh)]
+            for g in range(groups):
+                first = g == 0
+                last = g == groups - 1
+                pl, k = plane_of(g)
+                xr, xi, nxi = g, groups + g, 2 * groups + g
+                for j in range(nh):
+                    cr = NT * j
+                    ci = NT * (nh + j)
+                    mx(pos[j], m, xr, wts[g], cr, pl, k, cr, first, False)
+                    mx(pos[j], m, nxi, wts[g], ci, pl, k, ci, False, last)
+                    mx(neg[j], m, xr, wts[g], ci, pl, k, ci, first, False)
+                    mx(neg[j], m, xi, wts[g], cr, pl, k, cr, False, last)
+            o = keep.tile([P, 2 * nh * NT], F32, name="o%d" % m)
+            for j in range(nh):
+                nc.vector.tensor_copy(out=o[:, NT * j : NT * (j + 1)], in_=pos[j][:])
+                nc.scalar.copy(out=o[:, NT * (nh + j) : NT * (nh + j + 1)], in_=neg[j][:])
+            nc.scalar.dma_start(out=out[:, comp0 : comp0 + 2 * nh, :].rearrange("e c n -> e (c n)"), in_=o[:])
+
+        complex_phase(1, 6, 3, w1, lambda g: (planes["w1a"], 4 * g) if g < 4 else (planes["w1b"], 4 * (g - 4)), [6, 7, 0, 1, 2, 3], 4)
+        complex_phase(2, 4, 2, w2, lambda g: (planes["w2a"], 4 * g), [4, 5, 6, 7], 10)
+
+        y = [bank(j, "m0y%d" % j) for j in range(4)]
+        for g in range(8):
+            pl = planes["w0a"] if g < 4 else planes["w0b"]
+            k = 4 * (g % 4)
+            for j in range(4):
+                if g < 7:
+                    mx(y[j], 0, g, w0[g], NT * j, pl, k, NT * j, g == 0, False)
+                else:
+                    mx(y[j], 0, g, w0_last[j], 0, pl, k, NT * j, False, True)
+        o0 = keep.tile([P, 2048], F32, name="o0")
+        for j in range(4):
+            nc.vector.tensor_tensor(
+                out=o0[:, NT * j : NT * (j + 1)], in0=y[j][:], in1=bias[:, NT * j : NT * (j + 1)], op=mybir.AluOpType.add
+            )
+            nc.sync.dma_start(out=out[:, j, :], in_=o0[:, NT * j : NT * (j + 1)])

@@ -29,24 +29,30 @@ def tile_so2linear_w_kernel(tc, x, W0_words, W0_scales, b0, W1_words, W1_scales,
 
         ident = keep.tile([P, P], F32, name="ident")
         make_identity(nc, ident[:])
+
+        plane_specs = [
+            ("w1a", W1_scales, 0, 4, 3072, (0, 1, 2, 3)),
+            ("w1b", W1_scales, 4, 2, 3072, (0, 1, 2, 3)),
+            ("w2a", W2_scales, 0, 4, 2048, (2, 3, 0, 1)),
+            ("w0a", W0_scales, 0, 4, 2048, (2, 3, 0, 1)),
+            ("w0b", W0_scales, 4, 4, 2048, (2, 3, 0, 1)),
+        ]
+        planes = {}
+        for label, src, g0, ng, n, q_order in plane_specs:
+            pl = keep.tile([P, n], U8, name="pl_%s" % label, align_bytes=64)
+            nc.vector.memset(pl[:].bitcast(I32), 0)
+            planes[label] = pl
+            for q in q_order:
+                nc.gpsimd.dma_start(
+                    out=pl[32 * q : 32 * q + 4 * ng, :].bitcast(F32),
+                    in_=src[g0 : g0 + ng, 4 * q : 4 * q + 4, :].bitcast(F32),
+                )
+
         brow = keep.tile([P, 2048], BF16, name="brow")
         nc.vector.memset(brow[:].bitcast(I32), 0)
         ones = keep.tile([P, P], BF16, name="ones")
         nc.vector.memset(ones[:], 1.0)
         nc.scalar.dma_start(out=brow[0:1, :], in_=b0.rearrange("(o n) -> o n", o=1))
-
-        plane_specs = [
-            ("w1a", W1_scales, 0, 4, 3072),
-            ("w1b", W1_scales, 4, 2, 3072),
-            ("w2a", W2_scales, 0, 4, 2048),
-            ("w0a", W0_scales, 0, 4, 2048),
-            ("w0b", W0_scales, 4, 4, 2048),
-        ]
-        planes = {}
-        for label, src, g0, ng, n in plane_specs:
-            pl = keep.tile([P, n], U8, name="pl_%s" % label, align_bytes=64)
-            nc.vector.memset(pl[:].bitcast(I32), 0)
-            planes[label] = pl
 
         pieces = [(4, 7), (7, 10), (10, 14), (0, 4)]
         xp = []
@@ -54,14 +60,6 @@ def tile_so2linear_w_kernel(tc, x, W0_words, W0_scales, b0, W1_words, W1_scales,
             t = keep.tile([P, (c1 - c0) * 1024], BF16, name="xp%d" % i)
             nc.sync.dma_start(out=t[:], in_=x[:, c0:c1, :].rearrange("e c k -> e (c k)"))
             xp.append(t)
-
-        for label, src, g0, ng, n in plane_specs:
-            pl = planes[label]
-            for q in range(4):
-                nc.sync.dma_start(
-                    out=pl[32 * q : 32 * q + 4 * ng, :].bitcast(I32),
-                    in_=src[g0 : g0 + ng, 4 * q : 4 * q + 4, :].bitcast(I32),
-                )
 
         def load_w(words, g, n, label):
             t = wpool.tile([P, 3072], U32, tag="w", name="w_%s" % label, align_bytes=64)
@@ -84,8 +82,9 @@ def tile_so2linear_w_kernel(tc, x, W0_words, W0_scales, b0, W1_words, W1_scales,
             w0_last.append(t)
 
         bias = keep.tile([P, 2048], F32, name="bias")
-        for j in range(4):
-            bk = bank(4 + j, "bias%d" % j)
+
+        def spread_bias(j):
+            bk = bank(4 + j % 2, "bias%d" % j)
             nc.tensor.matmul(out=bk[:], lhsT=ones[:], rhs=brow[:, NT * j : NT * (j + 1)], start=True, stop=True)
             nc.scalar.copy(out=bias[:, NT * j : NT * (j + 1)], in_=bk[:])
 
@@ -160,6 +159,9 @@ def tile_so2linear_w_kernel(tc, x, W0_words, W0_scales, b0, W1_words, W1_scales,
                     mx(pos[j], m, nxi, wts[g], ci, pl, k, ci, False, last)
                     mx(neg[j], m, xr, wts[g], ci, pl, k, ci, first, False)
                     mx(neg[j], m, xi, wts[g], cr, pl, k, cr, False, last)
+                if m == 1 and g < 2:
+                    spread_bias(2 * g)
+                    spread_bias(2 * g + 1)
             o = keep.tile([P, 2 * nh * NT], F32, name="o%d" % m)
             for j in range(nh):
                 nc.vector.tensor_copy(out=o[:, NT * j : NT * (j + 1)], in_=pos[j][:])

@@ -71,15 +71,7 @@ def tile_so2linear_w_kernel(tc, x, W0_words, W0_scales, b0, W1_words, W1_scales,
 
         w1 = [load_w(W1_words, g, 3072, "1_%d" % g) for g in range(6)]
         w2 = [load_w(W2_words, g, 2048, "2_%d" % g) for g in range(4)]
-        w0 = [load_w(W0_words, g, 2048, "0_%d" % g) for g in range(7)]
-        w0_last = []
-        for j in range(4):
-            t = wpool.tile([P, NT], U32, tag="wl", bufs=4, name="wl_%d" % j, align_bytes=64)
-            nc.sync.dma_start(
-                out=t[:].bitcast(I32),
-                in_=W0_words[7].rearrange("p n t -> p (n t)")[:, 4 * NT * j : 4 * NT * (j + 1)].bitcast(I32),
-            )
-            w0_last.append(t)
+        w0 = [load_w(W0_words, g, 2048, "0_%d" % g) for g in range(8)]
 
         bias = keep.tile([P, 2048], F32, name="bias")
 
@@ -144,7 +136,9 @@ def tile_so2linear_w_kernel(tc, x, W0_words, W0_scales, b0, W1_words, W1_scales,
                 stop=stop,
             )
 
-        def complex_phase(m, groups, nh, wts, plane_of, banks, comp0):
+        o12 = keep.tile([P, 10 * NT], F32, name="o12")
+
+        def complex_phase(m, groups, nh, wts, plane_of, banks, col0):
             pos = [bank(banks[2 * j], "m%dpos%d" % (m, j)) for j in range(nh)]
             neg = [bank(banks[2 * j + 1], "m%dneg%d" % (m, j)) for j in range(nh)]
             for g in range(groups):
@@ -162,27 +156,26 @@ def tile_so2linear_w_kernel(tc, x, W0_words, W0_scales, b0, W1_words, W1_scales,
                 if m == 1 and g < 2:
                     spread_bias(2 * g)
                     spread_bias(2 * g + 1)
-            o = keep.tile([P, 2 * nh * NT], F32, name="o%d" % m)
             for j in range(nh):
-                nc.vector.tensor_copy(out=o[:, NT * j : NT * (j + 1)], in_=pos[j][:])
-                nc.scalar.copy(out=o[:, NT * (nh + j) : NT * (nh + j + 1)], in_=neg[j][:])
-            nc.scalar.dma_start(out=out[:, comp0 : comp0 + 2 * nh, :].rearrange("e c n -> e (c n)"), in_=o[:])
+                nc.vector.tensor_copy(out=o12[:, col0 + NT * j : col0 + NT * (j + 1)], in_=pos[j][:])
+                nc.scalar.copy(out=o12[:, col0 + NT * (nh + j) : col0 + NT * (nh + j + 1)], in_=neg[j][:])
 
-        complex_phase(1, 6, 3, w1, lambda g: (planes["w1a"], 4 * g) if g < 4 else (planes["w1b"], 4 * (g - 4)), [6, 7, 0, 1, 2, 3], 4)
-        complex_phase(2, 4, 2, w2, lambda g: (planes["w2a"], 4 * g), [4, 5, 6, 7], 10)
+        complex_phase(1, 6, 3, w1, lambda g: (planes["w1a"], 4 * g) if g < 4 else (planes["w1b"], 4 * (g - 4)), [6, 7, 0, 1, 2, 3], 0)
+        complex_phase(2, 4, 2, w2, lambda g: (planes["w2a"], 4 * g), [4, 5, 6, 7], 6 * NT)
+        nc.sync.dma_start(out=out[:, 4:14, :].rearrange("e c n -> e (c n)"), in_=o12[:])
 
         y = [bank(j, "m0y%d" % j) for j in range(4)]
         for g in range(8):
             pl = planes["w0a"] if g < 4 else planes["w0b"]
             k = 4 * (g % 4)
             for j in range(4):
-                if g < 7:
-                    mx(y[j], 0, g, w0[g], NT * j, pl, k, NT * j, g == 0, False)
-                else:
-                    mx(y[j], 0, g, w0_last[j], 0, pl, k, NT * j, False, True)
+                mx(y[j], 0, g, w0[g], NT * j, pl, k, NT * j, g == 0, g == 7)
         o0 = keep.tile([P, 2048], F32, name="o0")
         for j in range(4):
             nc.vector.tensor_tensor(
                 out=o0[:, NT * j : NT * (j + 1)], in0=y[j][:], in1=bias[:, NT * j : NT * (j + 1)], op=mybir.AluOpType.add
             )
-            nc.sync.dma_start(out=out[:, j, :], in_=o0[:, NT * j : NT * (j + 1)])
+            if j % 2 == 1:
+                nc.sync.dma_start(
+                    out=out[:, j - 1 : j + 1, :].rearrange("e c n -> e (c n)"), in_=o0[:, NT * (j - 1) : NT * (j + 1)]
+                )

@@ -31,22 +31,29 @@ def tile_so2linear_w_kernel(tc, x, W0_words, W0_scales, b0, W1_words, W1_scales,
         make_identity(nc, ident[:])
 
         plane_specs = [
-            ("w1a", W1_scales, 0, 4, 3072, (0, 1, 2, 3)),
-            ("w1b", W1_scales, 4, 2, 3072, (0, 1, 2, 3)),
-            ("w2a", W2_scales, 0, 4, 2048, (2, 3, 0, 1)),
-            ("w0a", W0_scales, 0, 4, 2048, (2, 3, 0, 1)),
-            ("w0b", W0_scales, 4, 4, 2048, (2, 3, 0, 1)),
+            ("w1a", W1_scales, 0, 4, 3072, (0, 1, 2, 3), False),
+            ("w1b", W1_scales, 4, 2, 3072, (0, 1, 2, 3), False),
+            ("w0b", W0_scales, 4, 4, 2048, (2, 3, 0, 1), False),
+            ("w2a", W2_scales, 0, 4, 2048, (0, 2, 1, 3), True),
+            ("w0a", W0_scales, 0, 4, 2048, (0, 2, 1, 3), True),
         ]
         planes = {}
-        for label, src, g0, ng, n, q_order in plane_specs:
+        for label, src, g0, ng, n, q_order, fine in plane_specs:
             pl = keep.tile([P, n], U8, name="pl_%s" % label, align_bytes=64)
             nc.vector.memset(pl[:].bitcast(I32), 0)
             planes[label] = pl
             for q in q_order:
-                nc.gpsimd.dma_start(
-                    out=pl[32 * q : 32 * q + 4 * ng, :].bitcast(F32),
-                    in_=src[g0 : g0 + ng, 4 * q : 4 * q + 4, :].bitcast(F32),
-                )
+                if fine:
+                    for r in range(4):
+                        nc.gpsimd.dma_start(
+                            out=pl[32 * q + r : 32 * q + 16 : 4, :].bitcast(F32),
+                            in_=src[g0 : g0 + ng, 4 * q + r, :].bitcast(F32),
+                        )
+                else:
+                    nc.gpsimd.dma_start(
+                        out=pl[32 * q : 32 * q + 4 * ng, :].bitcast(F32),
+                        in_=src[g0 : g0 + ng, 4 * q : 4 * q + 4, :].bitcast(F32),
+                    )
 
         brow = keep.tile([P, 2048], BF16, name="brow")
         nc.vector.memset(brow[:].bitcast(I32), 0)

@@ -30,30 +30,25 @@ def tile_so2linear_w_kernel(tc, x, W0_words, W0_scales, b0, W1_words, W1_scales,
         ident = keep.tile([P, P], F32, name="ident")
         make_identity(nc, ident[:])
 
-        plane_specs = [
-            ("w1a", W1_scales, 0, 4, 3072, (0, 1, 2, 3), False),
-            ("w1b", W1_scales, 4, 2, 3072, (0, 1, 2, 3), False),
-            ("w0b", W0_scales, 4, 4, 2048, (2, 3, 0, 1), False),
-            ("w2a", W2_scales, 0, 4, 2048, (0, 2, 1, 3), True),
-            ("w0a", W0_scales, 0, 4, 2048, (0, 2, 1, 3), True),
-        ]
+        plane_specs = {
+            "w1a": (W1_scales, 0, 4, 3072),
+            "w1b": (W1_scales, 4, 2, 3072),
+            "w2a": (W2_scales, 0, 4, 2048),
+            "w0a": (W0_scales, 0, 4, 2048),
+            "w0b": (W0_scales, 4, 4, 2048),
+        }
         planes = {}
-        for label, src, g0, ng, n, q_order, fine in plane_specs:
+        for label, (ssrc, g0, ng, n) in plane_specs.items():
             pl = keep.tile([P, n], U8, name="pl_%s" % label, align_bytes=64)
             nc.vector.memset(pl[:].bitcast(I32), 0)
             planes[label] = pl
-            for q in q_order:
-                if fine:
-                    for r in range(4):
-                        nc.gpsimd.dma_start(
-                            out=pl[32 * q + r : 32 * q + 16 : 4, :].bitcast(F32),
-                            in_=src[g0 : g0 + ng, 4 * q + r, :].bitcast(F32),
-                        )
-                else:
-                    nc.gpsimd.dma_start(
-                        out=pl[32 * q : 32 * q + 4 * ng, :].bitcast(F32),
-                        in_=src[g0 : g0 + ng, 4 * q : 4 * q + 4, :].bitcast(F32),
-                    )
+
+        def load_scales(label, q):
+            ssrc, g0, ng, n = plane_specs[label]
+            nc.sync.dma_start(
+                out=planes[label][32 * q : 32 * q + 4 * ng, :].bitcast(I32),
+                in_=ssrc[g0 : g0 + ng, 4 * q : 4 * q + 4, :].bitcast(I32),
+            )
 
         brow = keep.tile([P, 2048], BF16, name="brow")
         nc.vector.memset(brow[:].bitcast(I32), 0)
@@ -67,6 +62,9 @@ def tile_so2linear_w_kernel(tc, x, W0_words, W0_scales, b0, W1_words, W1_scales,
             t = keep.tile([P, (c1 - c0) * 1024], BF16, name="xp%d" % i)
             nc.sync.dma_start(out=t[:], in_=x[:, c0:c1, :].rearrange("e c k -> e (c k)"))
             xp.append(t)
+            if i > 0:
+                load_scales("w1a", i - 1)
+        load_scales("w1a", 3)
 
         def load_w(words, g, n, label):
             t = wpool.tile([P, 3072], U32, tag="w", name="w_%s" % label, align_bytes=64)
@@ -76,9 +74,23 @@ def tile_so2linear_w_kernel(tc, x, W0_words, W0_scales, b0, W1_words, W1_scales,
             )
             return t
 
-        w1 = [load_w(W1_words, g, 3072, "1_%d" % g) for g in range(6)]
-        w2 = [load_w(W2_words, g, 2048, "2_%d" % g) for g in range(4)]
-        w0 = [load_w(W0_words, g, 2048, "0_%d" % g) for g in range(8)]
+        w1 = []
+        w2 = []
+        w0 = []
+        for g in range(6):
+            w1.append(load_w(W1_words, g, 3072, "1_%d" % g))
+            if g < 4:
+                load_scales("w1b", g)
+            else:
+                load_scales("w2a", 2 * (g - 4))
+                load_scales("w2a", 2 * (g - 4) + 1)
+        for g in range(4):
+            w2.append(load_w(W2_words, g, 2048, "2_%d" % g))
+            load_scales("w0a", g)
+        for g in range(8):
+            w0.append(load_w(W0_words, g, 2048, "0_%d" % g))
+            if g < 4:
+                load_scales("w0b", g)
 
         bias = keep.tile([P, 2048], F32, name="bias")
 

@@ -45,9 +45,10 @@ def tile_so2linear_w_kernel(tc, x, W0_words, W0_scales, b0, W1_words, W1_scales,
 
         def load_scales(label, q):
             ssrc, g0, ng, n = plane_specs[label]
-            nc.sync.dma_start(
-                out=planes[label][32 * q : 32 * q + 4 * ng, :].bitcast(I32),
-                in_=ssrc[g0 : g0 + ng, 4 * q : 4 * q + 4, :].bitcast(I32),
+            queue, dt = (nc.sync, I32) if q < 2 else (nc.gpsimd, F32)
+            queue.dma_start(
+                out=planes[label][32 * q : 32 * q + 4 * ng, :].bitcast(dt),
+                in_=ssrc[g0 : g0 + ng, 4 * q : 4 * q + 4, :].bitcast(dt),
             )
 
         brow = keep.tile([P, 2048], BF16, name="brow")

@@ -88,10 +88,18 @@ def tile_so2linear_w_kernel(tc, x, W0_words, W0_scales, b0, W1_words, W1_scales,
         for g in range(4):
             w2.append(load_w(W2_words, g, 2048, "2_%d" % g))
             load_scales("w0a", g)
-        for g in range(8):
+        for g in range(6):
             w0.append(load_w(W0_words, g, 2048, "0_%d" % g))
             if g < 4:
                 load_scales("w0b", g)
+        for g in range(6, 8):
+            w0.append(wpool.tile([P, 3072], U32, tag="w", name="w_0_%d" % g, align_bytes=64))
+        for c in range(0, 2048, 1024):
+            for g in range(6, 8):
+                nc.sync.dma_start(
+                    out=w0[g][:, c : c + 1024].bitcast(I32),
+                    in_=W0_words[g, :, c : c + 1024, :].rearrange("p n t -> p (n t)").bitcast(I32),
+                )
 
         bias = keep.tile([P, 2048], F32, name="bias")
 
@@ -185,10 +193,10 @@ def tile_so2linear_w_kernel(tc, x, W0_words, W0_scales, b0, W1_words, W1_scales,
         nc.sync.dma_start(out=out[:, 4:14, :].rearrange("e c n -> e (c n)"), in_=o12[:])
 
         y = [bank(j, "m0y%d" % j) for j in range(4)]
-        for g in range(8):
+        for g, columns in [(g, range(4)) for g in range(6)] + [(6, (0, 1)), (7, (0, 1)), (6, (2, 3)), (7, (2, 3))]:
             pl = planes["w0a"] if g < 4 else planes["w0b"]
             k = 4 * (g % 4)
-            for j in range(4):
+            for j in columns:
                 mx(y[j], 0, g, w0[g], NT * j, pl, k, NT * j, g == 0, g == 7)
         o0 = keep.tile([P, 2048], F32, name="o0")
         for j in range(4):

from contextlib import ExitStack

import concourse.mybir as mybir
from concourse.masks import make_identity

F32 = mybir.dt.float32
BF16 = mybir.dt.bfloat16
I32 = mybir.dt.int32
U32 = mybir.dt.uint32
U8 = mybir.dt.uint8
FP8X4 = mybir.dt.float8_e4m3fn_x4

P = 128
NT = 512
FLOPS = 2 * 128 * (4096 * 2048 + 2 * 3072 * 3072 + 2 * 2048 * 2048)


def tile_so2linear_w_kernel(tc, x, W0_words, W0_scales, b0, W1_words, W1_scales, W2_words, W2_scales, out):
    nc = tc.nc
    with ExitStack() as ctx:
        ctx.enter_context(tc.manual_schedule())
        keep = ctx.enter_context(tc.tile_pool(name="keep", bufs=1))
        stage = ctx.enter_context(tc.tile_pool(name="stage", bufs=4))
        wpool = ctx.enter_context(tc.tile_pool(name="wpool", bufs=8))
        psum = ctx.enter_context(tc.psum_pool(name="psum", bufs=1))

        def bank(b, label):
            return psum.tile([P, NT], F32, tag="bank%d" % b, name="bk_%s" % label)

        ident = keep.tile([P, P], F32, name="ident")
        make_identity(nc, ident[:])

        plane_specs = {
            "w1a": (W1_scales, 0, 4, 3072),
            "w1b": (W1_scales, 4, 2, 3072),
            "w2a": (W2_scales, 0, 4, 2048),
            "w0a": (W0_scales, 0, 4, 2048),
            "w0b": (W0_scales, 4, 4, 2048),
        }
        planes = {}
        for label, (ssrc, g0, ng, n) in plane_specs.items():
            pl = keep.tile([P, n], U8, name="pl_%s" % label, align_bytes=64)
            nc.vector.memset(pl[:].bitcast(I32), 0)
            planes[label] = pl

        def load_scales(label, q):
            ssrc, g0, ng, n = plane_specs[label]
            queue, dt = (nc.sync, I32) if q < 2 else (nc.gpsimd, F32)
            queue.dma_start(
                out=planes[label][32 * q : 32 * q + 4 * ng, :].bitcast(dt),
                in_=ssrc[g0 : g0 + ng, 4 * q : 4 * q + 4, :].bitcast(dt),
            )

        brow = keep.tile([P, 2048], BF16, name="brow")
        nc.vector.memset(brow[:].bitcast(I32), 0)
        ones = keep.tile([P, P], BF16, name="ones")
        nc.vector.memset(ones[:], 1.0)
        nc.scalar.dma_start(out=brow[0:1, :], in_=b0.rearrange("(o n) -> o n", o=1))

        pieces = [(4, 7), (7, 10), (10, 14), (0, 4)]
        xp = []
        for i, (c0, c1) in enumerate(pieces):
            t = keep.tile([P, (c1 - c0) * 1024], BF16, name="xp%d" % i)
            nc.sync.dma_start(out=t[:], in_=x[:, c0:c1, :].rearrange("e c k -> e (c k)"))
            xp.append(t)
            if i > 0:
                load_scales("w1a", i - 1)
        load_scales("w1a", 3)

        def load_w(words, g, n, label):
            t = wpool.tile([P, 3072], U32, tag="w", name="w_%s" % label, align_bytes=64)
            nc.sync.dma_start(
                out=t[:, 0:n].bitcast(I32),
                in_=words[g].rearrange("p n t -> p (n t)").bitcast(I32),
            )
            return t

        w1 = []
        w2 = []
        w0 = []
        for g in range(6):
            w1.append(load_w(W1_words, g, 3072, "1_%d" % g))
            if g < 4:
                load_scales("w1b", g)
            else:
                load_scales("w2a", 2 * (g - 4))
                load_scales("w2a", 2 * (g - 4) + 1)
        for g in range(4):
            w2.append(load_w(W2_words, g, 2048, "2_%d" % g))
            load_scales("w0a", g)
        for g in range(6):
            w0.append(load_w(W0_words, g, 2048, "0_%d" % g))
            if g < 4:
                load_scales("w0b", g)
        for g in range(6, 8):
            w0.append(wpool.tile([P, 3072], U32, tag="w", name="w_0_%d" % g, align_bytes=64))
        for c in range(0, 2048, 1024):
            for g in range(6, 8):
                nc.sync.dma_start(
                    out=w0[g][:, c : c + 1024].bitcast(I32),
                    in_=W0_words[g, :, c : c + 1024, :].rearrange("p n t -> p (n t)").bitcast(I32),
                )

        bias = keep.tile([P, 2048], F32, name="bias")

        def spread_bias(j):
            bk = bank(4 + j % 2, "bias%d" % j)
            nc.tensor.matmul(out=bk[:], lhsT=ones[:], rhs=brow[:, NT * j : NT * (j + 1)], start=True, stop=True)
            nc.scalar.copy(out=bias[:, NT * j : NT * (j + 1)], in_=bk[:])

        n_slots = {1: 18, 2: 12, 0: 8}
        xq = {}
        xs = {}
        for m in (1, 2, 0):
            xq[m] = keep.tile([P, n_slots[m] * P], U32, name="xq%d" % m, align_bytes=64)
            xs[m] = keep.tile([P, n_slots[m] * P], U8, name="xs%d" % m, align_bytes=64)

        units = []
        for l in range(0, 6, 2):
            units.append((0, l, 1, l, None))
        for l in range(0, 6, 2):
            units.append((1, l, 1, 6 + l, 12 + l))
        for l in range(0, 4, 2):
            units.append((2, l, 2, l, None))
        for l in range(4, 8, 2):
            units.append((2, l, 2, l, 4 + l))
        for l in range(0, 8, 2):
            units.append((3, l, 0, l, None))

        def quantise(m, slot, src):
            nc.vector.quantize_mx(
                out=xq[m][:, slot * P : (slot + 2) * P].bitcast(FP8X4),
                scales=xs[m][:, slot * P : (slot + 2) * P],
                in_=src[:],
            )

        for i, (pc, l, m, slot, nslot) in enumerate(units):
            xw = xp[pc][:].bitcast(F32)
            bk = bank(i % 8, "t%d" % i)
            bk4 = bk[:].rearrange("p (j u e) -> p j u e", j=2, u=2)
            for j in range(2):
                for u in range(2):
                    nc.tensor.transpose(bk4[:, j, u, :], xw[:, 256 * (l + j) + u : 256 * (l + j + 1) : 2], ident[:])
            grp = stage.tile([P, 1024], BF16, tag="grp", name="grp%d" % i, align_bytes=64)
            nc.scalar.copy(
                out=grp[:].bitcast(F32).rearrange("p (j e u) -> p j e u", j=2, u=2),
                in_=bk4.rearrange("p j u e -> p j e u"),
            )
            if nslot is not None:
                neg = stage.tile([P, 1024], BF16, tag="neg", name="neg%d" % i, align_bytes=64)
                nc.vector.tensor_scalar(out=neg[:], in0=grp[:], scalar1=-1.0, scalar2=None, op0=mybir.AluOpType.mult)
            quantise(m, slot, grp)
            if nslot is not None:
                quantise(m, nslot, neg)

        def mx(acc, m, slot, wt, wcol, pl, k, pcol, start, stop):
            nc.tensor.matmul_mx(
                out=acc[:],
                lhsT=xq[m][:, slot * P : (slot + 1) * P].bitcast(FP8X4),
                lhsT_scale=xs[m][:, slot * P : (slot + 1) * P],
                rhs=wt[:, wcol : wcol + NT].bitcast(FP8X4),
                rhs_scale=pl[k:P, pcol : pcol + NT],
                start=start,
                stop=stop,
            )

        o12 = keep.tile([P, 10 * NT], F32, name="o12")

        def complex_phase(m, groups, nh, wts, plane_of, banks, col0):
            pos = [bank(banks[2 * j], "m%dpos%d" % (m, j)) for j in range(nh)]
            neg = [bank(banks[2 * j + 1], "m%dneg%d" % (m, j)) for j in range(nh)]
            for g in range(groups):
                first = g == 0
                last = g == groups - 1
                pl, k = plane_of(g)
                xr, xi, nxi = g, groups + g, 2 * groups + g
                for j in range(nh):
                    cr = NT * j
                    ci = NT * (nh + j)
                    mx(pos[j], m, xr, wts[g], cr, pl, k, cr, first, False)
                    mx(pos[j], m, nxi, wts[g], ci, pl, k, ci, False, last)
                    mx(neg[j], m, xr, wts[g], ci, pl, k, ci, first, False)
                    mx(neg[j], m, xi, wts[g], cr, pl, k, cr, False, last)
                if m == 1 and g < 2:
                    spread_bias(2 * g)
                    spread_bias(2 * g + 1)
            for j in range(nh):
                nc.vector.tensor_copy(out=o12[:, col0 + NT * j : col0 + NT * (j + 1)], in_=pos[j][:])
                nc.scalar.copy(out=o12[:, col0 + NT * (nh + j) : col0 + NT * (nh + j + 1)], in_=neg[j][:])

        complex_phase(1, 6, 3, w1, lambda g: (planes["w1a"], 4 * g) if g < 4 else (planes["w1b"], 4 * (g - 4)), [6, 7, 0, 1, 2, 3], 0)
        complex_phase(2, 4, 2, w2, lambda g: (planes["w2a"], 4 * g), [4, 5, 6, 7], 6 * NT)
        nc.sync.dma_start(out=out[:, 4:14, :].rearrange("e c n -> e (c n)"), in_=o12[:])

        y = [bank(j, "m0y%d" % j) for j in range(4)]
        for g, columns in [(g, range(4)) for g in range(6)] + [(6, (0, 1)), (7, (0, 1)), (6, (2, 3)), (7, (2, 3))]:
            pl = planes["w0a"] if g < 4 else planes["w0b"]
            k = 4 * (g % 4)
            for j in columns:
                mx(y[j], 0, g, w0[g], NT * j, pl, k, NT * j, g == 0, g == 7)
        o0 = keep.tile([P, 2048], F32, name="o0")
        for j in range(4):
            nc.vector.tensor_tensor(
                out=o0[:, NT * j : NT * (j + 1)], in0=y[j][:], in1=bias[:, NT * j : NT * (j + 1)], op=mybir.AluOpType.add
            )
            if j % 2 == 1:
                nc.sync.dma_start(
                    out=out[:, j - 1 : j + 1, :].rearrange("e c n -> e (c n)"), in_=o0[:, NT * (j - 1) : NT * (j + 1)]
                )
